import numpy as np
import ml_dtypes


def mxq(x, axis, fmt="e4m3"):
    dtype, down = {"e4m3": (ml_dtypes.float8_e4m3fn, 7), "e5m2": (ml_dtypes.float8_e5m2, 14)}[fmt]
    v = np.moveaxis(np.asarray(x, np.float32).astype(ml_dtypes.bfloat16).astype(np.float64), axis, -1)
    blocks = v.reshape(v.shape[:-1] + (-1, 32))
    amax = np.abs(blocks).max(-1, keepdims=True)
    byte = np.maximum(np.where(amax > 0, np.frexp(amax)[1] - 1 + 127, 0) - down, 1)
    scale = np.exp2(byte - 127.0)
    codes = (blocks / scale).astype(np.float32).astype(dtype).astype(np.float64)
    return np.moveaxis((codes * scale).reshape(v.shape), -1, axis)


WIDE = False


def mx_kscale(k):
    if not WIDE:
        return np.ones(k)
    levels = np.array([10, -10, 5, -5, 0])
    a = np.random.permutation(np.resize(levels, k // 512 * 4)).reshape(k // 512, 4)
    idx = np.arange(k)
    return np.exp2(a[idx // 512, idx % 128 // 32])


BF16 = ml_dtypes.bfloat16


def bf(x):
    return np.asarray(x, np.float32).astype(BF16)


def f64(x):
    return np.asarray(x).astype(np.float64)


E2M1 = np.array([0.0, 0.5, 1.0, 1.5, 2.0, 3.0, 4.0, 6.0, -0.0, -0.5, -1.0, -1.5, -2.0, -3.0, -4.0, -6.0])


def pack_weight(w, fmt):
    k, n = w.shape
    w = f64(bf(w)).reshape(k // 32, 32, n)
    amax = np.abs(w).max(1)
    if fmt == "e4m3":
        byte = np.frexp(amax)[1] - 1 + 127 - 7
    else:
        mant, ex = np.frexp(amax / 6.0)
        byte = np.where(mant > 0.5, ex, ex - 1) + 127
    byte = np.clip(np.where(amax > 0, byte, 1), 1, 254)
    scaled = (w * np.exp2(127.0 - byte)[:, None, :]).reshape(k, n).astype(np.float32)
    by_word = np.ascontiguousarray(scaled.reshape(k // 512, 128, 4, n).transpose(0, 1, 3, 2))
    if fmt == "e4m3":
        words = by_word.astype(ml_dtypes.float8_e4m3fn).view(np.uint8)
    else:
        c = by_word.astype(ml_dtypes.float4_e2m1fn).view(np.uint8) & 0xF
        words = c[..., 0::2] | (c[..., 1::2] << 4)
    return np.ascontiguousarray(words), np.ascontiguousarray(byte.astype(np.uint8).reshape(k // 512, 16, n))


def unpack_weight(words, scales, fmt):
    g, p, n, _ = words.shape
    if fmt == "e4m3":
        vals = np.ascontiguousarray(words).view(ml_dtypes.float8_e4m3fn).astype(np.float64)
    else:
        nib = np.empty((g, p, n, 4), np.uint8)
        nib[..., 0::2] = words & 0xF
        nib[..., 1::2] = words >> 4
        vals = E2M1[nib]
    vals = vals * np.repeat(np.exp2(scales.astype(np.float64) - 127.0), 8, axis=1)[..., None]
    return vals.transpose(0, 1, 3, 2).reshape(g * 512, n)


B, D, S, A, H, G = 4096, 512, 1024, 128, 512, 1
DG = D // G


def silu(v):
    return v / (1.0 + np.exp(-v))


def sigmoid(v):
    return 1.0 / (1.0 + np.exp(-v))


def setup_inputs():
    n = np.random.standard_normal
    t = mx_kscale(D)
    y_dyn = bf(silu(n((B, D))) * t)
    deter = bf(n((B, D)))
    stack = n((G, DG, 3 * DG)) * 2.0 / np.sqrt(DG) / t.reshape(G, DG)[:, :, None]
    words, scales = pack_weight(stack.reshape(-1, 3 * DG), "e4m3")
    gru_b = bf(n(3 * D) * 0.2)
    return {"y_dyn": y_dyn, "deter": deter, "gru_W_words": words, "gru_W_scales": scales, "gru_b": gru_b}


def reference(y_dyn, deter, gru_W_words, gru_W_scales, gru_b):
    yg = f64(y_dyn).reshape(B, G, DG).transpose(1, 0, 2)
    w = unpack_weight(gru_W_words, gru_W_scales, "e4m3").reshape(G, DG, 3 * DG)
    z = mxq(yg, 2, "e4m3") @ w
    z = z.transpose(1, 0, 2).reshape(B, 3 * D) + f64(gru_b)
    reset, cand, update = z[:, :D], z[:, D:2 * D], z[:, 2 * D:]
    reset = sigmoid(reset)
    cand = np.tanh(reset * cand)
    update = sigmoid(update - 1.0)
    return update * cand + (1.0 - update) * f64(deter)

@@ -1,0 +1,222 @@
+from contextlib import ExitStack
+
+import concourse.mybir as mybir
+from concourse.masks import make_identity
+
+F32 = mybir.dt.float32
+BF16 = mybir.dt.bfloat16
+I32 = mybir.dt.int32
+U32 = mybir.dt.uint32
+U8 = mybir.dt.uint8
+FP8X4 = mybir.dt.float8_e4m3fn_x4
+ACT = mybir.ActivationFunctionType
+ALU = mybir.AluOpType
+
+P = 128
+B = 4096
+D = 512
+GATES = 3
+RESET, CAND, UPDATE = 0, 1, 2
+CHUNK = 512
+CHUNKS = B // CHUNK
+ROWS = CHUNK // P
+FEATS = D // P
+UNITS = CHUNKS * FEATS
+
+FLOPS = 2 * B * D * GATES * D
+
+
+def tile_blockgrucell_pb_t_e_kernel(tc, y_dyn, deter, gru_W_words, gru_W_scales, gru_b, out):
+    nc = tc.nc
+    with ExitStack() as stack:
+        keep = stack.enter_context(tc.tile_pool(name="keep", bufs=1))
+        loads = stack.enter_context(tc.tile_pool(name="loads", bufs=CHUNKS))
+        group = stack.enter_context(tc.tile_pool(name="group", bufs=2))
+        codes = stack.enter_context(tc.tile_pool(name="codes", bufs=4))
+        work = stack.enter_context(tc.tile_pool(name="work", bufs=4))
+        psum_z = stack.enter_context(tc.psum_pool(name="psum_z", bufs=5))
+        psum_y = stack.enter_context(tc.psum_pool(name="psum_y", bufs=1))
+        psum_d = stack.enter_context(tc.psum_pool(name="psum_d", bufs=1))
+        psum_s = stack.enter_context(tc.psum_pool(name="psum_s", bufs=1))
+        stack.enter_context(tc.manual_schedule())
+
+        def chunk_rows(dram, c):
+            return dram[c * CHUNK : (c + 1) * CHUNK, :].rearrange("(p b) k -> p b k", b=ROWS)
+
+        w_scales = keep.tile([P, GATES * D], U8, align_bytes=64)
+        nc.vector.memset(w_scales[:].bitcast(I32), 0)
+        bias_rows = keep.tile([P, P], BF16)
+        nc.vector.memset(bias_rows[:], 0.0)
+        warm = keep.tile([P, 1], F32)
+        nc.vector.memset(warm[:], 0.0)
+        nc.scalar.activation(out=warm[:], in_=warm[:], func=ACT.Sigmoid)
+        ident_bf16 = keep.tile([P, P], BF16)
+        make_identity(nc, ident_bf16[:])
+        ident_f32 = keep.tile([P, P], F32)
+        make_identity(nc, ident_f32[:])
+
+        y_sb = []
+        deter_sb = []
+        for c in range(CHUNKS):
+            y_sb.append(loads.tile([P, ROWS, D], BF16, name="y_sb", tag="y"))
+            deter_sb.append(loads.tile([P, ROWS, D], BF16, name="deter_sb", tag="deter"))
+        w_codes = keep.tile([P, GATES * D], U32, align_bytes=64)
+
+        nc.sync.dma_start(out=bias_rows[0 : GATES * FEATS, :], in_=gru_b.rearrange("(r c) -> r c", c=P))
+        for half in range(2):
+            rows = slice(2 * half, 2 * half + 2)
+            nc.sync.dma_start(out=y_sb[0][:, rows, :], in_=chunk_rows(y_dyn, 0)[:, rows, :])
+        for quadrant in range(4):
+            nc.sync.dma_start(
+                out=w_scales[32 * quadrant : 32 * quadrant + 4, :].bitcast(I32),
+                in_=gru_W_scales[0, 4 * quadrant : 4 * quadrant + 4, :].bitcast(I32),
+            )
+        nc.sync.dma_start(
+            out=w_codes[:].bitcast(I32),
+            in_=gru_W_words[0].rearrange("p n t -> p (n t)").bitcast(I32),
+        )
+        for c in range(1, CHUNKS):
+            nc.sync.dma_start(out=y_sb[c][:], in_=chunk_rows(y_dyn, c))
+            nc.sync.dma_start(out=deter_sb[c - 1][:], in_=chunk_rows(deter, c - 1))
+        nc.sync.dma_start(out=deter_sb[CHUNKS - 1][:], in_=chunk_rows(deter, CHUNKS - 1))
+
+        bias_ps = psum_s.tile([P, P], BF16, tag="stepT")
+        nc.tensor.transpose(bias_ps[:], bias_rows[:], ident_bf16[:])
+        bias_cols = keep.tile([P, GATES * FEATS], F32)
+        nc.vector.tensor_copy(out=bias_cols[:], in_=bias_ps[:, 0 : GATES * FEATS])
+        update_cols = bias_cols[:, UPDATE * FEATS : (UPDATE + 1) * FEATS]
+        nc.vector.tensor_scalar_add(out=update_cols, in0=update_cols, scalar1=-1.0)
+
+        grouped = {}
+        y_codes = {}
+        y_scales = {}
+
+        def prepare_half(c, half):
+            if half == 0:
+                grouped[c] = group.tile([P, CHUNK, 4], BF16, name="grouped", align_bytes=64)
+            yT = psum_y.tile([P, 2, 2 * P], F32)
+            for b2 in range(2):
+                words = y_sb[c][:, 2 * half + b2, :].bitcast(F32)
+                for u in range(2):
+                    nc.tensor.transpose(yT[:, u, b2 * P : (b2 + 1) * P], words[:, u : D // 2 : 2], ident_f32[:])
+            pairs = grouped[c][:].rearrange("p b t -> p (b t)").bitcast(F32).rearrange("p (b u) -> p b u", u=2)
+            dst = pairs[:, half * 2 * P : (half + 1) * 2 * P, :]
+            src = yT[:].rearrange("p u b -> p b u")
+            if half == 0:
+                nc.scalar.copy(out=dst, in_=src)
+            else:
+                nc.vector.tensor_copy(out=dst, in_=src)
+
+        def quantise(c):
+            y_codes[c] = codes.tile([P, CHUNK], U32, name="y_codes", align_bytes=64)
+            y_scales[c] = codes.tile([P, CHUNK], U8, name="y_scales", align_bytes=64)
+            nc.vector.quantize_mx(
+                out=y_codes[c][:].bitcast(FP8X4),
+                scales=y_scales[c][:],
+                in_=grouped[c][:].rearrange("p b t -> p (b t)"),
+            )
+
+        def prepare_third(c, third):
+            if c < CHUNKS:
+                if third < 2:
+                    prepare_half(c, third)
+                else:
+                    quantise(c)
+
+        z = {}
+        deterT = {}
+        reset = {}
+        update = {}
+        gated = {}
+        cand = {}
+        diff = {}
+        step = {}
+        stepT = {}
+
+        def bias_of(gate, n):
+            col = gate * FEATS + n % FEATS
+            return bias_cols[:, col : col + 1]
+
+        def project(n):
+            c, j = divmod(n, FEATS)
+            for gate in range(GATES):
+                z[gate, n] = psum_z.tile([P, CHUNK], F32, name="z", tag="z")
+                cols = slice(gate * D + j * P, gate * D + (j + 1) * P)
+                nc.tensor.matmul_mx(
+                    out=z[gate, n][:],
+                    lhsT=w_codes[:, cols].bitcast(FP8X4),
+                    lhsT_scale=w_scales[:, cols],
+                    rhs=y_codes[c][:].bitcast(FP8X4),
+                    rhs_scale=y_scales[c][:],
+                    start=True,
+                    stop=True,
+                )
+
+        def transpose_deter(n):
+            c, j = divmod(n, FEATS)
+            deterT[n] = psum_d.tile([P, CHUNK], F32, name="deterT")
+            for b in range(ROWS):
+                nc.tensor.matmul(
+                    out=deterT[n][:, b * P : (b + 1) * P],
+                    lhsT=deter_sb[c][:, b, j * P : (j + 1) * P],
+                    rhs=ident_bf16[:],
+                    start=True,
+                    stop=True,
+                )
+
+        def reset_gate(n):
+            reset[n] = work.tile([P, CHUNK], F32, name="reset")
+            nc.scalar.activation(out=reset[n][:], in_=z[RESET, n][:], func=ACT.Sigmoid, bias=bias_of(RESET, n), scale=1.0)
+
+        def update_gate(n):
+            update[n] = work.tile([P, CHUNK], F32, name="update")
+            nc.scalar.activation(out=update[n][:], in_=z[UPDATE, n][:], func=ACT.Sigmoid, bias=bias_of(UPDATE, n), scale=1.0)
+
+        def gate_candidate(n):
+            gated[n] = work.tile([P, CHUNK], F32, name="gated")
+            nc.vector.scalar_tensor_tensor(
+                out=gated[n][:], in0=z[CAND, n][:], scalar=bias_of(CAND, n), in1=reset[n][:], op0=ALU.add, op1=ALU.mult
+            )
+
+        def candidate(n):
+            cand[n] = work.tile([P, CHUNK], F32, name="cand")
+            nc.scalar.activation(out=cand[n][:], in_=gated[n][:], func=ACT.Tanh)
+
+        def difference(n):
+            diff[n] = work.tile([P, CHUNK], F32, name="diff")
+            nc.vector.tensor_tensor(out=diff[n][:], in0=cand[n][:], in1=deterT[n][:], op=ALU.subtract)
+
+        def weighted_step(n):
+            step[n] = work.tile([P, CHUNK], F32, name="step")
+            nc.gpsimd.tensor_tensor(out=step[n][:], in0=update[n][:], in1=diff[n][:], op=ALU.mult)
+
+        def transpose_step(n):
+            stepT[n] = psum_s.tile([P, ROWS, P], F32, name="stepT", tag="stepT")
+            for b in range(ROWS):
+                nc.tensor.transpose(stepT[n][:, b, :], step[n][:, b * P : (b + 1) * P], ident_f32[:])
+
+        def blend_and_store(n):
+            c, j = divmod(n, FEATS)
+            feats = slice(j * P, (j + 1) * P)
+            result = work.tile([P, ROWS, P], F32, name="result")
+            nc.vector.tensor_tensor(out=result[:], in0=stepT[n][:], in1=deter_sb[c][:, :, feats], op=ALU.add)
+            nc.sync.dma_start(out=chunk_rows(out, c)[:, :, feats], in_=result[:])
+
+        def at(stage, n):
+            if 0 <= n < UNITS:
+                stage(n)
+
+        for third in range(3):
+            prepare_third(0, third)
+        for t in range(UNITS + 4):
+            prepare_third(1 + t // 3, t % 3)
+            at(blend_and_store, t - 4)
+            at(project, t)
+            at(transpose_deter, t - 1)
+            at(transpose_step, t - 3)
+            at(reset_gate, t)
+            at(candidate, t - 1)
+            at(update_gate, t)
+            at(gate_candidate, t)
+            at(difference, t - 1)
+            at(weighted_step, t - 1)

@@ -34,10 +34,7 @@ def tile_blockgrucell_pb_t_e_kernel(tc, y_dyn, deter, gru_W_words, gru_W_scales,
         group = stack.enter_context(tc.tile_pool(name="group", bufs=2))
         codes = stack.enter_context(tc.tile_pool(name="codes", bufs=4))
         work = stack.enter_context(tc.tile_pool(name="work", bufs=4))
-        psum_z = stack.enter_context(tc.psum_pool(name="psum_z", bufs=5))
-        psum_y = stack.enter_context(tc.psum_pool(name="psum_y", bufs=1))
-        psum_d = stack.enter_context(tc.psum_pool(name="psum_d", bufs=1))
-        psum_s = stack.enter_context(tc.psum_pool(name="psum_s", bufs=1))
+        psum = stack.enter_context(tc.psum_pool(name="psum", bufs=8))
         stack.enter_context(tc.manual_schedule())
 
         def chunk_rows(dram, c):
@@ -80,7 +77,7 @@ def tile_blockgrucell_pb_t_e_kernel(tc, y_dyn, deter, gru_W_words, gru_W_scales,
             nc.sync.dma_start(out=deter_sb[c - 1][:], in_=chunk_rows(deter, c - 1))
         nc.sync.dma_start(out=deter_sb[CHUNKS - 1][:], in_=chunk_rows(deter, CHUNKS - 1))
 
-        bias_ps = psum_s.tile([P, P], BF16, tag="stepT")
+        bias_ps = psum.tile([P, P], BF16, tag="bank")
         nc.tensor.transpose(bias_ps[:], bias_rows[:], ident_bf16[:])
         bias_cols = keep.tile([P, GATES * FEATS], F32)
         nc.vector.tensor_copy(out=bias_cols[:], in_=bias_ps[:, 0 : GATES * FEATS])
@@ -94,7 +91,7 @@ def tile_blockgrucell_pb_t_e_kernel(tc, y_dyn, deter, gru_W_words, gru_W_scales,
         def prepare_half(c, half):
             if half == 0:
                 grouped[c] = group.tile([P, CHUNK, 4], BF16, name="grouped", align_bytes=64)
-            yT = psum_y.tile([P, 2, 2 * P], F32)
+            yT = psum.tile([P, 2, 2 * P], F32, tag="bank")
             for b2 in range(2):
                 words = y_sb[c][:, 2 * half + b2, :].bitcast(F32)
                 for u in range(2):
@@ -140,7 +137,7 @@ def tile_blockgrucell_pb_t_e_kernel(tc, y_dyn, deter, gru_W_words, gru_W_scales,
         def project(n):
             c, j = divmod(n, FEATS)
             for gate in range(GATES):
-                z[gate, n] = psum_z.tile([P, CHUNK], F32, name="z", tag="z")
+                z[gate, n] = psum.tile([P, CHUNK], F32, name="z", tag="bank")
                 cols = slice(gate * D + j * P, gate * D + (j + 1) * P)
                 nc.tensor.matmul_mx(
                     out=z[gate, n][:],
@@ -154,7 +151,7 @@ def tile_blockgrucell_pb_t_e_kernel(tc, y_dyn, deter, gru_W_words, gru_W_scales,
 
         def transpose_deter(n):
             c, j = divmod(n, FEATS)
-            deterT[n] = psum_d.tile([P, CHUNK], F32, name="deterT")
+            deterT[n] = psum.tile([P, CHUNK], F32, name="deterT", tag="bank")
             for b in range(ROWS):
                 nc.tensor.matmul(
                     out=deterT[n][:, b * P : (b + 1) * P],
@@ -191,7 +188,7 @@ def tile_blockgrucell_pb_t_e_kernel(tc, y_dyn, deter, gru_W_words, gru_W_scales,
             nc.gpsimd.tensor_tensor(out=step[n][:], in0=update[n][:], in1=diff[n][:], op=ALU.mult)
 
         def transpose_step(n):
-            stepT[n] = psum_s.tile([P, ROWS, P], F32, name="stepT", tag="stepT")
+            stepT[n] = psum.tile([P, ROWS, P], F32, name="stepT", tag="bank")
             for b in range(ROWS):
                 nc.tensor.transpose(stepT[n][:, b, :], step[n][:, b * P : (b + 1) * P], ident_f32[:])
 

@@ -13,6 +13,7 @@ ACT = mybir.ActivationFunctionType
 ALU = mybir.AluOpType
 
 P = 128
+PACK = 4
 B = 4096
 D = 512
 GATES = 3
@@ -20,8 +21,16 @@ RESET, CAND, UPDATE = 0, 1, 2
 CHUNK = 512
 CHUNKS = B // CHUNK
 ROWS = CHUNK // P
+HALF = CHUNK // 2
 FEATS = D // P
 UNITS = CHUNKS * FEATS
+PSUM_BANKS = 8
+
+LAG_CAND = 1
+LAG_BACK = 3
+LAG_OUT = 4
+
+PREPARE_STEPS = 3
 
 FLOPS = 2 * B * D * GATES * D
 
@@ -33,8 +42,8 @@ def tile_blockgrucell_pb_t_e_kernel(tc, y_dyn, deter, gru_W_words, gru_W_scales,
         loads = stack.enter_context(tc.tile_pool(name="loads", bufs=CHUNKS))
         group = stack.enter_context(tc.tile_pool(name="group", bufs=2))
         codes = stack.enter_context(tc.tile_pool(name="codes", bufs=4))
-        work = stack.enter_context(tc.tile_pool(name="work", bufs=4))
-        psum = stack.enter_context(tc.psum_pool(name="psum", bufs=8))
+        work = stack.enter_context(tc.tile_pool(name="work", bufs=LAG_BACK + 1))
+        psum = stack.enter_context(tc.psum_pool(name="psum", bufs=PSUM_BANKS))
         stack.enter_context(tc.manual_schedule())
 
         def chunk_rows(dram, c):
@@ -61,8 +70,9 @@ def tile_blockgrucell_pb_t_e_kernel(tc, y_dyn, deter, gru_W_words, gru_W_scales,
 
         nc.sync.dma_start(out=bias_rows[0 : GATES * FEATS, :], in_=gru_b.rearrange("(r c) -> r c", c=P))
         for half in range(2):
-            rows = slice(2 * half, 2 * half + 2)
+            rows = slice(half * ROWS // 2, (half + 1) * ROWS // 2)
             nc.sync.dma_start(out=y_sb[0][:, rows, :], in_=chunk_rows(y_dyn, 0)[:, rows, :])
+        nc.sync.dma_start(out=y_sb[1][:], in_=chunk_rows(y_dyn, 1))
         for quadrant in range(4):
             nc.sync.dma_start(
                 out=w_scales[32 * quadrant : 32 * quadrant + 4, :].bitcast(I32),
@@ -72,10 +82,11 @@ def tile_blockgrucell_pb_t_e_kernel(tc, y_dyn, deter, gru_W_words, gru_W_scales,
             out=w_codes[:].bitcast(I32),
             in_=gru_W_words[0].rearrange("p n t -> p (n t)").bitcast(I32),
         )
-        for c in range(1, CHUNKS):
+        for c in range(2, CHUNKS):
             nc.sync.dma_start(out=y_sb[c][:], in_=chunk_rows(y_dyn, c))
-            nc.sync.dma_start(out=deter_sb[c - 1][:], in_=chunk_rows(deter, c - 1))
-        nc.sync.dma_start(out=deter_sb[CHUNKS - 1][:], in_=chunk_rows(deter, CHUNKS - 1))
+            nc.sync.dma_start(out=deter_sb[c - 2][:], in_=chunk_rows(deter, c - 2))
+        for c in range(CHUNKS - 2, CHUNKS):
+            nc.sync.dma_start(out=deter_sb[c][:], in_=chunk_rows(deter, c))
 
         bias_ps = psum.tile([P, P], BF16, tag="bank")
         nc.tensor.transpose(bias_ps[:], bias_rows[:], ident_bf16[:])
@@ -88,16 +99,16 @@ def tile_blockgrucell_pb_t_e_kernel(tc, y_dyn, deter, gru_W_words, gru_W_scales,
         y_codes = {}
         y_scales = {}
 
-        def prepare_half(c, half):
+        def transpose_half(c, half):
             if half == 0:
-                grouped[c] = group.tile([P, CHUNK, 4], BF16, name="grouped", align_bytes=64)
-            yT = psum.tile([P, 2, 2 * P], F32, tag="bank")
-            for b2 in range(2):
-                words = y_sb[c][:, 2 * half + b2, :].bitcast(F32)
+                grouped[c] = group.tile([P, CHUNK, PACK], BF16, name="grouped", align_bytes=64)
+            yT = psum.tile([P, 2, HALF], F32, tag="bank")
+            for i in range(HALF // P):
+                words = y_sb[c][:, half * HALF // P + i, :].bitcast(F32)
                 for u in range(2):
-                    nc.tensor.transpose(yT[:, u, b2 * P : (b2 + 1) * P], words[:, u : D // 2 : 2], ident_f32[:])
+                    nc.tensor.transpose(yT[:, u, i * P : (i + 1) * P], words[:, u : D // 2 : 2], ident_f32[:])
             pairs = grouped[c][:].rearrange("p b t -> p (b t)").bitcast(F32).rearrange("p (b u) -> p b u", u=2)
-            dst = pairs[:, half * 2 * P : (half + 1) * 2 * P, :]
+            dst = pairs[:, half * HALF : (half + 1) * HALF, :]
             src = yT[:].rearrange("p u b -> p b u")
             if half == 0:
                 nc.scalar.copy(out=dst, in_=src)
@@ -113,10 +124,10 @@ def tile_blockgrucell_pb_t_e_kernel(tc, y_dyn, deter, gru_W_words, gru_W_scales,
                 in_=grouped[c][:].rearrange("p b t -> p (b t)"),
             )
 
-        def prepare_third(c, third):
+        def prepare(c, prepare_step):
             if c < CHUNKS:
-                if third < 2:
-                    prepare_half(c, third)
+                if prepare_step < 2:
+                    transpose_half(c, prepare_step)
                 else:
                     quantise(c)
 
@@ -149,18 +160,6 @@ def tile_blockgrucell_pb_t_e_kernel(tc, y_dyn, deter, gru_W_words, gru_W_scales,
                     stop=True,
                 )
 
-        def transpose_deter(n):
-            c, j = divmod(n, FEATS)
-            deterT[n] = psum.tile([P, CHUNK], F32, name="deterT", tag="bank")
-            for b in range(ROWS):
-                nc.tensor.matmul(
-                    out=deterT[n][:, b * P : (b + 1) * P],
-                    lhsT=deter_sb[c][:, b, j * P : (j + 1) * P],
-                    rhs=ident_bf16[:],
-                    start=True,
-                    stop=True,
-                )
-
         def reset_gate(n):
             reset[n] = work.tile([P, CHUNK], F32, name="reset")
             nc.scalar.activation(out=reset[n][:], in_=z[RESET, n][:], func=ACT.Sigmoid, bias=bias_of(RESET, n), scale=1.0)
@@ -178,6 +177,18 @@ def tile_blockgrucell_pb_t_e_kernel(tc, y_dyn, deter, gru_W_words, gru_W_scales,
         def candidate(n):
             cand[n] = work.tile([P, CHUNK], F32, name="cand")
             nc.scalar.activation(out=cand[n][:], in_=gated[n][:], func=ACT.Tanh)
+
+        def transpose_deter(n):
+            c, j = divmod(n, FEATS)
+            deterT[n] = psum.tile([P, CHUNK], F32, name="deterT", tag="bank")
+            for b in range(ROWS):
+                nc.tensor.matmul(
+                    out=deterT[n][:, b * P : (b + 1) * P],
+                    lhsT=deter_sb[c][:, b, j * P : (j + 1) * P],
+                    rhs=ident_bf16[:],
+                    start=True,
+                    stop=True,
+                )
 
         def difference(n):
             diff[n] = work.tile([P, CHUNK], F32, name="diff")
@@ -203,17 +214,17 @@ def tile_blockgrucell_pb_t_e_kernel(tc, y_dyn, deter, gru_W_words, gru_W_scales,
             if 0 <= n < UNITS:
                 stage(n)
 
-        for third in range(3):
-            prepare_third(0, third)
-        for t in range(UNITS + 4):
-            prepare_third(1 + t // 3, t % 3)
-            at(blend_and_store, t - 4)
+        for prepare_step in range(PREPARE_STEPS):
+            prepare(0, prepare_step)
+        for t in range(UNITS + LAG_OUT):
+            prepare(1 + t // PREPARE_STEPS, t % PREPARE_STEPS)
+            at(blend_and_store, t - LAG_OUT)
             at(project, t)
-            at(transpose_deter, t - 1)
-            at(transpose_step, t - 3)
+            at(transpose_deter, t - LAG_CAND)
+            at(transpose_step, t - LAG_BACK)
             at(reset_gate, t)
-            at(candidate, t - 1)
+            at(candidate, t - LAG_CAND)
             at(update_gate, t)
             at(gate_candidate, t)
-            at(difference, t - 1)
-            at(weighted_step, t - 1)
+            at(difference, t - LAG_CAND)
+            at(weighted_step, t - LAG_CAND)

@@ -56,10 +56,10 @@ def tile_blockgrucell_pb_t_e_kernel(tc, y_dyn, deter, gru_W_words, gru_W_scales,
         warm = keep.tile([P, 1], F32)
         nc.vector.memset(warm[:], 0.0)
         nc.scalar.activation(out=warm[:], in_=warm[:], func=ACT.Sigmoid)
-        ident_bf16 = keep.tile([P, P], BF16)
-        make_identity(nc, ident_bf16[:])
         ident_f32 = keep.tile([P, P], F32)
         make_identity(nc, ident_f32[:])
+        ident_bf16 = keep.tile([P, P], BF16)
+        make_identity(nc, ident_bf16[:])
 
         y_sb = []
         deter_sb = []
@@ -68,10 +68,10 @@ def tile_blockgrucell_pb_t_e_kernel(tc, y_dyn, deter, gru_W_words, gru_W_scales,
             deter_sb.append(loads.tile([P, ROWS, D], BF16, name="deter_sb", tag="deter"))
         w_codes = keep.tile([P, GATES * D], U32, align_bytes=64)
 
-        nc.sync.dma_start(out=bias_rows[0 : GATES * FEATS, :], in_=gru_b.rearrange("(r c) -> r c", c=P))
         for half in range(2):
             rows = slice(half * ROWS // 2, (half + 1) * ROWS // 2)
             nc.sync.dma_start(out=y_sb[0][:, rows, :], in_=chunk_rows(y_dyn, 0)[:, rows, :])
+        nc.sync.dma_start(out=bias_rows[0 : GATES * FEATS, :], in_=gru_b.rearrange("(r c) -> r c", c=P))
         nc.sync.dma_start(out=y_sb[1][:], in_=chunk_rows(y_dyn, 1))
         for quadrant in range(4):
             nc.sync.dma_start(
@@ -87,13 +87,6 @@ def tile_blockgrucell_pb_t_e_kernel(tc, y_dyn, deter, gru_W_words, gru_W_scales,
             nc.sync.dma_start(out=deter_sb[c - 2][:], in_=chunk_rows(deter, c - 2))
         for c in range(CHUNKS - 2, CHUNKS):
             nc.sync.dma_start(out=deter_sb[c][:], in_=chunk_rows(deter, c))
-
-        bias_ps = psum.tile([P, P], BF16, tag="bank")
-        nc.tensor.transpose(bias_ps[:], bias_rows[:], ident_bf16[:])
-        bias_cols = keep.tile([P, GATES * FEATS], F32)
-        nc.vector.tensor_copy(out=bias_cols[:], in_=bias_ps[:, 0 : GATES * FEATS])
-        update_cols = bias_cols[:, UPDATE * FEATS : (UPDATE + 1) * FEATS]
-        nc.vector.tensor_scalar_add(out=update_cols, in0=update_cols, scalar1=-1.0)
 
         grouped = {}
         y_codes = {}
@@ -196,7 +189,8 @@ def tile_blockgrucell_pb_t_e_kernel(tc, y_dyn, deter, gru_W_words, gru_W_scales,
 
         def weighted_step(n):
             step[n] = work.tile([P, CHUNK], F32, name="step")
-            nc.gpsimd.tensor_tensor(out=step[n][:], in0=update[n][:], in1=diff[n][:], op=ALU.mult)
+            engine = nc.vector if n == UNITS - 1 else nc.gpsimd
+            engine.tensor_tensor(out=step[n][:], in0=update[n][:], in1=diff[n][:], op=ALU.mult)
 
         def transpose_step(n):
             stepT[n] = psum.tile([P, ROWS, P], F32, name="stepT", tag="bank")
@@ -216,6 +210,13 @@ def tile_blockgrucell_pb_t_e_kernel(tc, y_dyn, deter, gru_W_words, gru_W_scales,
 
         for prepare_step in range(PREPARE_STEPS):
             prepare(0, prepare_step)
+
+        bias_ps = psum.tile([P, P], BF16, tag="bank")
+        nc.tensor.transpose(bias_ps[:], bias_rows[:], ident_bf16[:])
+        bias_cols = keep.tile([P, GATES * FEATS], F32)
+        nc.vector.tensor_copy(out=bias_cols[:], in_=bias_ps[:, 0 : GATES * FEATS])
+        update_cols = bias_cols[:, UPDATE * FEATS : (UPDATE + 1) * FEATS]
+        nc.vector.tensor_scalar_add(out=update_cols, in0=update_cols, scalar1=-1.0)
         for t in range(UNITS + LAG_OUT):
             prepare(1 + t // PREPARE_STEPS, t % PREPARE_STEPS)
             at(blend_and_store, t - LAG_OUT)

@@ -72,37 +72,47 @@ def tile_blockgrucell_pb_t_e_kernel(tc, y_dyn, deter, gru_W_words, gru_W_scales,
             rows = slice(half * ROWS // 2, (half + 1) * ROWS // 2)
             nc.sync.dma_start(out=y_sb[0][:, rows, :], in_=chunk_rows(y_dyn, 0)[:, rows, :])
         nc.sync.dma_start(out=bias_rows[0 : GATES * FEATS, :], in_=gru_b.rearrange("(r c) -> r c", c=P))
-        nc.sync.dma_start(out=y_sb[1][:], in_=chunk_rows(y_dyn, 1))
         for quadrant in range(4):
             nc.sync.dma_start(
                 out=w_scales[32 * quadrant : 32 * quadrant + 4, :].bitcast(I32),
                 in_=gru_W_scales[0, 4 * quadrant : 4 * quadrant + 4, :].bitcast(I32),
             )
-        nc.sync.dma_start(
-            out=w_codes[:].bitcast(I32),
-            in_=gru_W_words[0].rearrange("p n t -> p (n t)").bitcast(I32),
-        )
+        by_tile = "p (g j w) -> p g j w"
+        codes_sbuf = w_codes[:].bitcast(I32).rearrange(by_tile, g=GATES, j=FEATS)
+        codes_dram = gru_W_words[0].rearrange("p n t -> p (n t)").bitcast(I32).rearrange(by_tile, g=GATES, j=FEATS)
+
+        def load_codes(j):
+            nc.sync.dma_start(out=codes_sbuf[:, :, j, :], in_=codes_dram[:, :, j, :])
+
+        load_codes(0)
+        load_codes(1)
+        nc.sync.dma_start(out=y_sb[1][:], in_=chunk_rows(y_dyn, 1))
+        nc.sync.dma_start(out=deter_sb[0][:], in_=chunk_rows(deter, 0))
+        load_codes(2)
+        load_codes(3)
         for c in range(2, CHUNKS):
             nc.sync.dma_start(out=y_sb[c][:], in_=chunk_rows(y_dyn, c))
-            nc.sync.dma_start(out=deter_sb[c - 2][:], in_=chunk_rows(deter, c - 2))
-        for c in range(CHUNKS - 2, CHUNKS):
-            nc.sync.dma_start(out=deter_sb[c][:], in_=chunk_rows(deter, c))
+            nc.sync.dma_start(out=deter_sb[c - 1][:], in_=chunk_rows(deter, c - 1))
+        nc.sync.dma_start(out=deter_sb[CHUNKS - 1][:], in_=chunk_rows(deter, CHUNKS - 1))
 
         grouped = {}
+        yT = {}
         y_codes = {}
         y_scales = {}
 
         def transpose_half(c, half):
             if half == 0:
                 grouped[c] = group.tile([P, CHUNK, PACK], BF16, name="grouped", align_bytes=64)
-            yT = psum.tile([P, 2, HALF], F32, tag="bank")
+            yT[c, half] = psum.tile([P, 2, HALF], F32, name="yT", tag="bank")
             for i in range(HALF // P):
                 words = y_sb[c][:, half * HALF // P + i, :].bitcast(F32)
                 for u in range(2):
-                    nc.tensor.transpose(yT[:, u, i * P : (i + 1) * P], words[:, u : D // 2 : 2], ident_f32[:])
+                    nc.tensor.transpose(yT[c, half][:, u, i * P : (i + 1) * P], words[:, u : D // 2 : 2], ident_f32[:])
+
+        def empty_half(c, half):
             pairs = grouped[c][:].rearrange("p b t -> p (b t)").bitcast(F32).rearrange("p (b u) -> p b u", u=2)
             dst = pairs[:, half * HALF : (half + 1) * HALF, :]
-            src = yT[:].rearrange("p u b -> p b u")
+            src = yT[c, half][:].rearrange("p u b -> p b u")
             if half == 0:
                 nc.scalar.copy(out=dst, in_=src)
             else:
@@ -117,10 +127,14 @@ def tile_blockgrucell_pb_t_e_kernel(tc, y_dyn, deter, gru_W_words, gru_W_scales,
                 in_=grouped[c][:].rearrange("p b t -> p (b t)"),
             )
 
-        def prepare(c, prepare_step):
+        def prepare_on_tensor(c, prepare_step):
+            if c < CHUNKS and prepare_step < 2:
+                transpose_half(c, prepare_step)
+
+        def prepare_elsewhere(c, prepare_step):
             if c < CHUNKS:
                 if prepare_step < 2:
-                    transpose_half(c, prepare_step)
+                    empty_half(c, prepare_step)
                 else:
                     quantise(c)
 
@@ -209,7 +223,8 @@ def tile_blockgrucell_pb_t_e_kernel(tc, y_dyn, deter, gru_W_words, gru_W_scales,
                 stage(n)
 
         for prepare_step in range(PREPARE_STEPS):
-            prepare(0, prepare_step)
+            prepare_on_tensor(0, prepare_step)
+            prepare_elsewhere(0, prepare_step)
 
         bias_ps = psum.tile([P, P], BF16, tag="bank")
         nc.tensor.transpose(bias_ps[:], bias_rows[:], ident_bf16[:])
@@ -218,14 +233,15 @@ def tile_blockgrucell_pb_t_e_kernel(tc, y_dyn, deter, gru_W_words, gru_W_scales,
         update_cols = bias_cols[:, UPDATE * FEATS : (UPDATE + 1) * FEATS]
         nc.vector.tensor_scalar_add(out=update_cols, in0=update_cols, scalar1=-1.0)
         for t in range(UNITS + LAG_OUT):
-            prepare(1 + t // PREPARE_STEPS, t % PREPARE_STEPS)
             at(blend_and_store, t - LAG_OUT)
             at(project, t)
             at(transpose_deter, t - LAG_CAND)
             at(transpose_step, t - LAG_BACK)
+            prepare_on_tensor(1 + t // PREPARE_STEPS, t % PREPARE_STEPS)
             at(reset_gate, t)
             at(candidate, t - LAG_CAND)
             at(update_gate, t)
             at(gate_candidate, t)
             at(difference, t - LAG_CAND)
             at(weighted_step, t - LAG_CAND)
+            prepare_elsewhere(1 + t // PREPARE_STEPS, t % PREPARE_STEPS)

@@ -71,26 +71,17 @@ def tile_blockgrucell_pb_t_e_kernel(tc, y_dyn, deter, gru_W_words, gru_W_scales,
         for half in range(2):
             rows = slice(half * ROWS // 2, (half + 1) * ROWS // 2)
             nc.sync.dma_start(out=y_sb[0][:, rows, :], in_=chunk_rows(y_dyn, 0)[:, rows, :])
-        nc.sync.dma_start(out=bias_rows[0 : GATES * FEATS, :], in_=gru_b.rearrange("(r c) -> r c", c=P))
+        nc.sync.dma_start(
+            out=w_codes[:].bitcast(I32),
+            in_=gru_W_words[0].rearrange("p n t -> p (n t)").bitcast(I32),
+        )
         for quadrant in range(4):
             nc.sync.dma_start(
                 out=w_scales[32 * quadrant : 32 * quadrant + 4, :].bitcast(I32),
                 in_=gru_W_scales[0, 4 * quadrant : 4 * quadrant + 4, :].bitcast(I32),
             )
-        by_tile = "p (g j w) -> p g j w"
-        codes_sbuf = w_codes[:].bitcast(I32).rearrange(by_tile, g=GATES, j=FEATS)
-        codes_dram = gru_W_words[0].rearrange("p n t -> p (n t)").bitcast(I32).rearrange(by_tile, g=GATES, j=FEATS)
-
-        def load_codes(j):
-            nc.sync.dma_start(out=codes_sbuf[:, :, j, :], in_=codes_dram[:, :, j, :])
-
-        load_codes(0)
-        load_codes(1)
-        nc.sync.dma_start(out=y_sb[1][:], in_=chunk_rows(y_dyn, 1))
-        nc.sync.dma_start(out=deter_sb[0][:], in_=chunk_rows(deter, 0))
-        load_codes(2)
-        load_codes(3)
-        for c in range(2, CHUNKS):
+        nc.sync.dma_start(out=bias_rows[0 : GATES * FEATS, :], in_=gru_b.rearrange("(r c) -> r c", c=P))
+        for c in range(1, CHUNKS):
             nc.sync.dma_start(out=y_sb[c][:], in_=chunk_rows(y_dyn, c))
             nc.sync.dma_start(out=deter_sb[c - 1][:], in_=chunk_rows(deter, c - 1))
         nc.sync.dma_start(out=deter_sb[CHUNKS - 1][:], in_=chunk_rows(deter, CHUNKS - 1))

@@ -23,7 +23,9 @@ CHUNKS = B // CHUNK
 ROWS = CHUNK // P
 HALF = CHUNK // 2
 FEATS = D // P
-UNITS = CHUNKS * FEATS
+TAIL_SPLIT = 1
+VECTOR_STEPS = 3
+SCALAR_BLENDS = 3
 PSUM_BANKS = 8
 
 LAG_CAND = 1
@@ -45,6 +47,16 @@ def tile_blockgrucell_pb_t_e_kernel(tc, y_dyn, deter, gru_W_words, gru_W_scales,
         work = stack.enter_context(tc.tile_pool(name="work", bufs=LAG_BACK + 1))
         psum = stack.enter_context(tc.psum_pool(name="psum", bufs=PSUM_BANKS))
         stack.enter_context(tc.manual_schedule())
+
+        units = []
+        for c in range(CHUNKS):
+            for j in range(FEATS):
+                if c == CHUNKS - 1 and j >= FEATS - TAIL_SPLIT:
+                    units.append((c, j, 0, HALF))
+                    units.append((c, j, HALF, HALF))
+                else:
+                    units.append((c, j, 0, CHUNK))
+        UNITS = len(units)
 
         def chunk_rows(dram, c):
             return dram[c * CHUNK : (c + 1) * CHUNK, :].rearrange("(p b) k -> p b k", b=ROWS)
@@ -71,18 +83,20 @@ def tile_blockgrucell_pb_t_e_kernel(tc, y_dyn, deter, gru_W_words, gru_W_scales,
         for half in range(2):
             rows = slice(half * ROWS // 2, (half + 1) * ROWS // 2)
             nc.sync.dma_start(out=y_sb[0][:, rows, :], in_=chunk_rows(y_dyn, 0)[:, rows, :])
+        nc.sync.dma_start(out=y_sb[1][:], in_=chunk_rows(y_dyn, 1))
         nc.sync.dma_start(
             out=w_codes[:].bitcast(I32),
             in_=gru_W_words[0].rearrange("p n t -> p (n t)").bitcast(I32),
         )
+        nc.sync.dma_start(out=bias_rows[0 : GATES * FEATS, :], in_=gru_b.rearrange("(r c) -> r c", c=P))
         for quadrant in range(4):
             nc.sync.dma_start(
                 out=w_scales[32 * quadrant : 32 * quadrant + 4, :].bitcast(I32),
                 in_=gru_W_scales[0, 4 * quadrant : 4 * quadrant + 4, :].bitcast(I32),
             )
-        nc.sync.dma_start(out=bias_rows[0 : GATES * FEATS, :], in_=gru_b.rearrange("(r c) -> r c", c=P))
         for c in range(1, CHUNKS):
-            nc.sync.dma_start(out=y_sb[c][:], in_=chunk_rows(y_dyn, c))
+            if c > 1:
+                nc.sync.dma_start(out=y_sb[c][:], in_=chunk_rows(y_dyn, c))
             nc.sync.dma_start(out=deter_sb[c - 1][:], in_=chunk_rows(deter, c - 1))
         nc.sync.dma_start(out=deter_sb[CHUNKS - 1][:], in_=chunk_rows(deter, CHUNKS - 1))
 
@@ -104,7 +118,7 @@ def tile_blockgrucell_pb_t_e_kernel(tc, y_dyn, deter, gru_W_words, gru_W_scales,
             pairs = grouped[c][:].rearrange("p b t -> p (b t)").bitcast(F32).rearrange("p (b u) -> p b u", u=2)
             dst = pairs[:, half * HALF : (half + 1) * HALF, :]
             src = yT[c, half][:].rearrange("p u b -> p b u")
-            if half == 0:
+            if half == 0 or c == 1:
                 nc.scalar.copy(out=dst, in_=src)
             else:
                 nc.vector.tensor_copy(out=dst, in_=src)
@@ -140,48 +154,57 @@ def tile_blockgrucell_pb_t_e_kernel(tc, y_dyn, deter, gru_W_words, gru_W_scales,
         stepT = {}
 
         def bias_of(gate, n):
-            col = gate * FEATS + n % FEATS
+            col = gate * FEATS + units[n][1]
             return bias_cols[:, col : col + 1]
 
+        def width_of(n):
+            return units[n][3]
+
+        def row_blocks(n):
+            return range(units[n][2] // P, (units[n][2] + units[n][3]) // P)
+
+        def on_scalar(n):
+            return UNITS - 2 * TAIL_SPLIT - SCALAR_BLENDS <= n < UNITS - 2 * TAIL_SPLIT
+
         def project(n):
-            c, j = divmod(n, FEATS)
+            c, j, first, width = units[n]
             for gate in range(GATES):
-                z[gate, n] = psum.tile([P, CHUNK], F32, name="z", tag="bank")
+                z[gate, n] = psum.tile([P, width], F32, name="z", tag="bank")
                 cols = slice(gate * D + j * P, gate * D + (j + 1) * P)
                 nc.tensor.matmul_mx(
                     out=z[gate, n][:],
                     lhsT=w_codes[:, cols].bitcast(FP8X4),
                     lhsT_scale=w_scales[:, cols],
-                    rhs=y_codes[c][:].bitcast(FP8X4),
-                    rhs_scale=y_scales[c][:],
+                    rhs=y_codes[c][:, first : first + width].bitcast(FP8X4),
+                    rhs_scale=y_scales[c][:, first : first + width],
                     start=True,
                     stop=True,
                 )
 
         def reset_gate(n):
-            reset[n] = work.tile([P, CHUNK], F32, name="reset")
+            reset[n] = work.tile([P, width_of(n)], F32, name="reset")
             nc.scalar.activation(out=reset[n][:], in_=z[RESET, n][:], func=ACT.Sigmoid, bias=bias_of(RESET, n), scale=1.0)
 
         def update_gate(n):
-            update[n] = work.tile([P, CHUNK], F32, name="update")
+            update[n] = work.tile([P, width_of(n)], F32, name="update")
             nc.scalar.activation(out=update[n][:], in_=z[UPDATE, n][:], func=ACT.Sigmoid, bias=bias_of(UPDATE, n), scale=1.0)
 
         def gate_candidate(n):
-            gated[n] = work.tile([P, CHUNK], F32, name="gated")
+            gated[n] = work.tile([P, width_of(n)], F32, name="gated")
             nc.vector.scalar_tensor_tensor(
                 out=gated[n][:], in0=z[CAND, n][:], scalar=bias_of(CAND, n), in1=reset[n][:], op0=ALU.add, op1=ALU.mult
             )
 
         def candidate(n):
-            cand[n] = work.tile([P, CHUNK], F32, name="cand")
+            cand[n] = work.tile([P, width_of(n)], F32, name="cand")
             nc.scalar.activation(out=cand[n][:], in_=gated[n][:], func=ACT.Tanh)
 
         def transpose_deter(n):
-            c, j = divmod(n, FEATS)
-            deterT[n] = psum.tile([P, CHUNK], F32, name="deterT", tag="bank")
-            for b in range(ROWS):
+            c, j = units[n][0], units[n][1]
+            deterT[n] = psum.tile([P, width_of(n)], F32, name="deterT", tag="bank")
+            for i, b in enumerate(row_blocks(n)):
                 nc.tensor.matmul(
-                    out=deterT[n][:, b * P : (b + 1) * P],
+                    out=deterT[n][:, i * P : (i + 1) * P],
                     lhsT=deter_sb[c][:, b, j * P : (j + 1) * P],
                     rhs=ident_bf16[:],
                     start=True,
@@ -189,33 +212,56 @@ def tile_blockgrucell_pb_t_e_kernel(tc, y_dyn, deter, gru_W_words, gru_W_scales,
                 )
 
         def difference(n):
-            diff[n] = work.tile([P, CHUNK], F32, name="diff")
+            diff[n] = work.tile([P, width_of(n)], F32, name="diff")
             nc.vector.tensor_tensor(out=diff[n][:], in0=cand[n][:], in1=deterT[n][:], op=ALU.subtract)
 
         def weighted_step(n):
-            step[n] = work.tile([P, CHUNK], F32, name="step")
-            engine = nc.vector if n == UNITS - 1 else nc.gpsimd
+            step[n] = work.tile([P, width_of(n)], F32, name="step")
+            engine = nc.vector if n >= UNITS - VECTOR_STEPS else nc.gpsimd
             engine.tensor_tensor(out=step[n][:], in0=update[n][:], in1=diff[n][:], op=ALU.mult)
 
         def transpose_step(n):
-            stepT[n] = psum.tile([P, ROWS, P], F32, name="stepT", tag="bank")
-            for b in range(ROWS):
-                nc.tensor.transpose(stepT[n][:, b, :], step[n][:, b * P : (b + 1) * P], ident_f32[:])
+            c, j = units[n][0], units[n][1]
+            stepT[n] = psum.tile([P, width_of(n) // P, P], F32, name="stepT", tag="bank")
+            for i, b in enumerate(row_blocks(n)):
+                if on_scalar(n):
+                    nc.tensor.matmul(
+                        out=stepT[n][:, i, :],
+                        lhsT=ident_bf16[:],
+                        rhs=deter_sb[c][:, b, j * P : (j + 1) * P],
+                        start=True,
+                        stop=False,
+                    )
+                    nc.tensor.matmul(
+                        out=stepT[n][:, i, :],
+                        lhsT=step[n][:, i * P : (i + 1) * P],
+                        rhs=ident_f32[:],
+                        is_transpose=True,
+                        start=False,
+                        stop=True,
+                    )
+                else:
+                    nc.tensor.transpose(stepT[n][:, i, :], step[n][:, i * P : (i + 1) * P], ident_f32[:])
 
         def blend_and_store(n):
-            c, j = divmod(n, FEATS)
+            c, j = units[n][0], units[n][1]
             feats = slice(j * P, (j + 1) * P)
-            result = work.tile([P, ROWS, P], F32, name="result")
-            nc.vector.tensor_tensor(out=result[:], in0=stepT[n][:], in1=deter_sb[c][:, :, feats], op=ALU.add)
-            nc.sync.dma_start(out=chunk_rows(out, c)[:, :, feats], in_=result[:])
+            rows = slice(row_blocks(n).start, row_blocks(n).stop)
+            result = work.tile([P, width_of(n) // P, P], F32, name="result")
+            if on_scalar(n):
+                nc.scalar.copy(out=result[:], in_=stepT[n][:])
+            else:
+                nc.vector.tensor_tensor(out=result[:], in0=stepT[n][:], in1=deter_sb[c][:, rows, feats], op=ALU.add)
+            nc.sync.dma_start(out=chunk_rows(out, c)[:, rows, feats], in_=result[:])
 
         def at(stage, n):
             if 0 <= n < UNITS:
                 stage(n)
 
-        for prepare_step in range(PREPARE_STEPS):
-            prepare_on_tensor(0, prepare_step)
-            prepare_elsewhere(0, prepare_step)
+        for c in range(2):
+            for prepare_step in range(PREPARE_STEPS):
+                prepare_on_tensor(c, prepare_step)
+                prepare_elsewhere(c, prepare_step)
 
         bias_ps = psum.tile([P, P], BF16, tag="bank")
         nc.tensor.transpose(bias_ps[:], bias_rows[:], ident_bf16[:])
@@ -224,15 +270,21 @@ def tile_blockgrucell_pb_t_e_kernel(tc, y_dyn, deter, gru_W_words, gru_W_scales,
         update_cols = bias_cols[:, UPDATE * FEATS : (UPDATE + 1) * FEATS]
         nc.vector.tensor_scalar_add(out=update_cols, in0=update_cols, scalar1=-1.0)
         for t in range(UNITS + LAG_OUT):
-            at(blend_and_store, t - LAG_OUT)
+            if not on_scalar(t - LAG_OUT):
+                at(blend_and_store, t - LAG_OUT)
             at(project, t)
             at(transpose_deter, t - LAG_CAND)
             at(transpose_step, t - LAG_BACK)
-            prepare_on_tensor(1 + t // PREPARE_STEPS, t % PREPARE_STEPS)
+            prepare_on_tensor(2 + t // PREPARE_STEPS, t % PREPARE_STEPS)
             at(reset_gate, t)
             at(candidate, t - LAG_CAND)
-            at(update_gate, t)
+            if t != UNITS - 1:
+                at(update_gate, t)
+            if t == UNITS:
+                update_gate(UNITS - 1)
+            if on_scalar(t - LAG_OUT):
+                blend_and_store(t - LAG_OUT)
             at(gate_candidate, t)
             at(difference, t - LAG_CAND)
             at(weighted_step, t - LAG_CAND)
-            prepare_elsewhere(1 + t // PREPARE_STEPS, t % PREPARE_STEPS)
+            prepare_elsewhere(2 + t // PREPARE_STEPS, t % PREPARE_STEPS)

@@ -94,11 +94,10 @@ def tile_blockgrucell_pb_t_e_kernel(tc, y_dyn, deter, gru_W_words, gru_W_scales,
                 out=w_scales[32 * quadrant : 32 * quadrant + 4, :].bitcast(I32),
                 in_=gru_W_scales[0, 4 * quadrant : 4 * quadrant + 4, :].bitcast(I32),
             )
-        for c in range(1, CHUNKS):
-            if c > 1:
-                nc.sync.dma_start(out=y_sb[c][:], in_=chunk_rows(y_dyn, c))
-            nc.sync.dma_start(out=deter_sb[c - 1][:], in_=chunk_rows(deter, c - 1))
-        nc.sync.dma_start(out=deter_sb[CHUNKS - 1][:], in_=chunk_rows(deter, CHUNKS - 1))
+        for c in range(CHUNKS):
+            if c + 2 < CHUNKS:
+                nc.sync.dma_start(out=y_sb[c + 2][:], in_=chunk_rows(y_dyn, c + 2))
+            nc.sync.dma_start(out=deter_sb[c][:], in_=chunk_rows(deter, c))
 
         grouped = {}
         yT = {}

@@ -117,7 +117,7 @@ def tile_blockgrucell_pb_t_e_kernel(tc, y_dyn, deter, gru_W_words, gru_W_scales,
             pairs = grouped[c][:].rearrange("p b t -> p (b t)").bitcast(F32).rearrange("p (b u) -> p b u", u=2)
             dst = pairs[:, half * HALF : (half + 1) * HALF, :]
             src = yT[c, half][:].rearrange("p u b -> p b u")
-            if half == 0 or c == 1:
+            if (half == 0 and c != 2) or c == 1:
                 nc.scalar.copy(out=dst, in_=src)
             else:
                 nc.vector.tensor_copy(out=dst, in_=src)

@@ -34,6 +34,11 @@ LAG_OUT = 4
 
 PREPARE_STEPS = 3
 
+EARLY_CHUNKS = 2
+Y_AHEAD = 4
+DETER_AHEAD = 4
+OUT_BUFFERS = 8
+
 FLOPS = 2 * B * D * GATES * D
 
 
@@ -45,6 +50,7 @@ def tile_blockgrucell_pb_t_e_kernel(tc, y_dyn, deter, gru_W_words, gru_W_scales,
         group = stack.enter_context(tc.tile_pool(name="group", bufs=2))
         codes = stack.enter_context(tc.tile_pool(name="codes", bufs=4))
         work = stack.enter_context(tc.tile_pool(name="work", bufs=LAG_BACK + 1))
+        outs = stack.enter_context(tc.tile_pool(name="outs", bufs=OUT_BUFFERS))
         psum = stack.enter_context(tc.psum_pool(name="psum", bufs=PSUM_BANKS))
         stack.enter_context(tc.manual_schedule())
 
@@ -94,10 +100,23 @@ def tile_blockgrucell_pb_t_e_kernel(tc, y_dyn, deter, gru_W_words, gru_W_scales,
                 out=w_scales[32 * quadrant : 32 * quadrant + 4, :].bitcast(I32),
                 in_=gru_W_scales[0, 4 * quadrant : 4 * quadrant + 4, :].bitcast(I32),
             )
-        for c in range(CHUNKS):
-            if c + 2 < CHUNKS:
-                nc.sync.dma_start(out=y_sb[c + 2][:], in_=chunk_rows(y_dyn, c + 2))
+        def load_y(c):
+            nc.sync.dma_start(out=y_sb[c][:], in_=chunk_rows(y_dyn, c))
+
+        def load_deter(c):
             nc.sync.dma_start(out=deter_sb[c][:], in_=chunk_rows(deter, c))
+
+        for c in range(EARLY_CHUNKS):
+            load_y(c + 2)
+            load_deter(c)
+
+        def load_later(t):
+            c, rest = divmod(t + Y_AHEAD, PREPARE_STEPS)
+            if rest == 0 and EARLY_CHUNKS <= c < CHUNKS - 2:
+                load_y(c + 2)
+            c, rest = divmod(t + DETER_AHEAD, FEATS)
+            if rest == 0 and EARLY_CHUNKS <= c < CHUNKS:
+                load_deter(c)
 
         grouped = {}
         yT = {}
@@ -246,7 +265,7 @@ def tile_blockgrucell_pb_t_e_kernel(tc, y_dyn, deter, gru_W_words, gru_W_scales,
             c, j = units[n][0], units[n][1]
             feats = slice(j * P, (j + 1) * P)
             rows = slice(row_blocks(n).start, row_blocks(n).stop)
-            result = work.tile([P, width_of(n) // P, P], F32, name="result")
+            result = outs.tile([P, width_of(n) // P, P], F32, name="result")
             if on_scalar(n):
                 nc.scalar.copy(out=result[:], in_=stepT[n][:])
             else:
@@ -269,6 +288,7 @@ def tile_blockgrucell_pb_t_e_kernel(tc, y_dyn, deter, gru_W_words, gru_W_scales,
         update_cols = bias_cols[:, UPDATE * FEATS : (UPDATE + 1) * FEATS]
         nc.vector.tensor_scalar_add(out=update_cols, in0=update_cols, scalar1=-1.0)
         for t in range(UNITS + LAG_OUT):
+            load_later(t)
             if not on_scalar(t - LAG_OUT):
                 at(blend_and_store, t - LAG_OUT)
             at(project, t)

from contextlib import ExitStack

import concourse.mybir as mybir
from concourse.masks import make_identity

F32 = mybir.dt.float32
BF16 = mybir.dt.bfloat16
I32 = mybir.dt.int32
U32 = mybir.dt.uint32
U8 = mybir.dt.uint8
FP8X4 = mybir.dt.float8_e4m3fn_x4
ACT = mybir.ActivationFunctionType
ALU = mybir.AluOpType

P = 128
PACK = 4
B = 4096
D = 512
GATES = 3
RESET, CAND, UPDATE = 0, 1, 2
CHUNK = 512
CHUNKS = B // CHUNK
ROWS = CHUNK // P
HALF = CHUNK // 2
FEATS = D // P
TAIL_SPLIT = 1
VECTOR_STEPS = 3
SCALAR_BLENDS = 3
PSUM_BANKS = 8

LAG_CAND = 1
LAG_BACK = 3
LAG_OUT = 4

PREPARE_STEPS = 3

EARLY_CHUNKS = 2
Y_AHEAD = 4
DETER_AHEAD = 4
OUT_BUFFERS = 8

FLOPS = 2 * B * D * GATES * D


def tile_blockgrucell_pb_t_e_kernel(tc, y_dyn, deter, gru_W_words, gru_W_scales, gru_b, out):
    nc = tc.nc
    with ExitStack() as stack:
        keep = stack.enter_context(tc.tile_pool(name="keep", bufs=1))
        loads = stack.enter_context(tc.tile_pool(name="loads", bufs=CHUNKS))
        group = stack.enter_context(tc.tile_pool(name="group", bufs=2))
        codes = stack.enter_context(tc.tile_pool(name="codes", bufs=4))
        work = stack.enter_context(tc.tile_pool(name="work", bufs=LAG_BACK + 1))
        outs = stack.enter_context(tc.tile_pool(name="outs", bufs=OUT_BUFFERS))
        psum = stack.enter_context(tc.psum_pool(name="psum", bufs=PSUM_BANKS))
        stack.enter_context(tc.manual_schedule())

        units = []
        for c in range(CHUNKS):
            for j in range(FEATS):
                if c == CHUNKS - 1 and j >= FEATS - TAIL_SPLIT:
                    units.append((c, j, 0, HALF))
                    units.append((c, j, HALF, HALF))
                else:
                    units.append((c, j, 0, CHUNK))
        UNITS = len(units)

        def chunk_rows(dram, c):
            return dram[c * CHUNK : (c + 1) * CHUNK, :].rearrange("(p b) k -> p b k", b=ROWS)

        w_scales = keep.tile([P, GATES * D], U8, align_bytes=64)
        nc.vector.memset(w_scales[:].bitcast(I32), 0)
        bias_rows = keep.tile([P, P], BF16)
        nc.vector.memset(bias_rows[:], 0.0)
        warm = keep.tile([P, 1], F32)
        nc.vector.memset(warm[:], 0.0)
        nc.scalar.activation(out=warm[:], in_=warm[:], func=ACT.Sigmoid)
        ident_f32 = keep.tile([P, P], F32)
        make_identity(nc, ident_f32[:])
        ident_bf16 = keep.tile([P, P], BF16)
        make_identity(nc, ident_bf16[:])

        y_sb = []
        deter_sb = []
        for c in range(CHUNKS):
            y_sb.append(loads.tile([P, ROWS, D], BF16, name="y_sb", tag="y"))
            deter_sb.append(loads.tile([P, ROWS, D], BF16, name="deter_sb", tag="deter"))
        w_codes = keep.tile([P, GATES * D], U32, align_bytes=64)

        for half in range(2):
            rows = slice(half * ROWS // 2, (half + 1) * ROWS // 2)
            nc.sync.dma_start(out=y_sb[0][:, rows, :], in_=chunk_rows(y_dyn, 0)[:, rows, :])
        nc.sync.dma_start(out=y_sb[1][:], in_=chunk_rows(y_dyn, 1))
        nc.sync.dma_start(
            out=w_codes[:].bitcast(I32),
            in_=gru_W_words[0].rearrange("p n t -> p (n t)").bitcast(I32),
        )
        nc.sync.dma_start(out=bias_rows[0 : GATES * FEATS, :], in_=gru_b.rearrange("(r c) -> r c", c=P))
        for quadrant in range(4):
            nc.sync.dma_start(
                out=w_scales[32 * quadrant : 32 * quadrant + 4, :].bitcast(I32),
                in_=gru_W_scales[0, 4 * quadrant : 4 * quadrant + 4, :].bitcast(I32),
            )
        def load_y(c):
            nc.sync.dma_start(out=y_sb[c][:], in_=chunk_rows(y_dyn, c))

        def load_deter(c):
            nc.sync.dma_start(out=deter_sb[c][:], in_=chunk_rows(deter, c))

        for c in range(EARLY_CHUNKS):
            load_y(c + 2)
            load_deter(c)

        def load_later(t):
            c, rest = divmod(t + Y_AHEAD, PREPARE_STEPS)
            if rest == 0 and EARLY_CHUNKS <= c < CHUNKS - 2:
                load_y(c + 2)
            c, rest = divmod(t + DETER_AHEAD, FEATS)
            if rest == 0 and EARLY_CHUNKS <= c < CHUNKS:
                load_deter(c)

        grouped = {}
        yT = {}
        y_codes = {}
        y_scales = {}

        def transpose_half(c, half):
            if half == 0:
                grouped[c] = group.tile([P, CHUNK, PACK], BF16, name="grouped", align_bytes=64)
            yT[c, half] = psum.tile([P, 2, HALF], F32, name="yT", tag="bank")
            for i in range(HALF // P):
                words = y_sb[c][:, half * HALF // P + i, :].bitcast(F32)
                for u in range(2):
                    nc.tensor.transpose(yT[c, half][:, u, i * P : (i + 1) * P], words[:, u : D // 2 : 2], ident_f32[:])

        def empty_half(c, half):
            pairs = grouped[c][:].rearrange("p b t -> p (b t)").bitcast(F32).rearrange("p (b u) -> p b u", u=2)
            dst = pairs[:, half * HALF : (half + 1) * HALF, :]
            src = yT[c, half][:].rearrange("p u b -> p b u")
            if (half == 0 and c != 2) or c == 1:
                nc.scalar.copy(out=dst, in_=src)
            else:
                nc.vector.tensor_copy(out=dst, in_=src)

        def quantise(c):
            y_codes[c] = codes.tile([P, CHUNK], U32, name="y_codes", align_bytes=64)
            y_scales[c] = codes.tile([P, CHUNK], U8, name="y_scales", align_bytes=64)
            nc.vector.quantize_mx(
                out=y_codes[c][:].bitcast(FP8X4),
                scales=y_scales[c][:],
                in_=grouped[c][:].rearrange("p b t -> p (b t)"),
            )

        def prepare_on_tensor(c, prepare_step):
            if c < CHUNKS and prepare_step < 2:
                transpose_half(c, prepare_step)

        def prepare_elsewhere(c, prepare_step):
            if c < CHUNKS:
                if prepare_step < 2:
                    empty_half(c, prepare_step)
                else:
                    quantise(c)

        z = {}
        deterT = {}
        reset = {}
        update = {}
        gated = {}
        cand = {}
        diff = {}
        step = {}
        stepT = {}

        def bias_of(gate, n):
            col = gate * FEATS + units[n][1]
            return bias_cols[:, col : col + 1]

        def width_of(n):
            return units[n][3]

        def row_blocks(n):
            return range(units[n][2] // P, (units[n][2] + units[n][3]) // P)

        def on_scalar(n):
            return UNITS - 2 * TAIL_SPLIT - SCALAR_BLENDS <= n < UNITS - 2 * TAIL_SPLIT

        def project(n):
            c, j, first, width = units[n]
            for gate in range(GATES):
                z[gate, n] = psum.tile([P, width], F32, name="z", tag="bank")
                cols = slice(gate * D + j * P, gate * D + (j + 1) * P)
                nc.tensor.matmul_mx(
                    out=z[gate, n][:],
                    lhsT=w_codes[:, cols].bitcast(FP8X4),
                    lhsT_scale=w_scales[:, cols],
                    rhs=y_codes[c][:, first : first + width].bitcast(FP8X4),
                    rhs_scale=y_scales[c][:, first : first + width],
                    start=True,
                    stop=True,
                )

        def reset_gate(n):
            reset[n] = work.tile([P, width_of(n)], F32, name="reset")
            nc.scalar.activation(out=reset[n][:], in_=z[RESET, n][:], func=ACT.Sigmoid, bias=bias_of(RESET, n), scale=1.0)

        def update_gate(n):
            update[n] = work.tile([P, width_of(n)], F32, name="update")
            nc.scalar.activation(out=update[n][:], in_=z[UPDATE, n][:], func=ACT.Sigmoid, bias=bias_of(UPDATE, n), scale=1.0)

        def gate_candidate(n):
            gated[n] = work.tile([P, width_of(n)], F32, name="gated")
            nc.vector.scalar_tensor_tensor(
                out=gated[n][:], in0=z[CAND, n][:], scalar=bias_of(CAND, n), in1=reset[n][:], op0=ALU.add, op1=ALU.mult
            )

        def candidate(n):
            cand[n] = work.tile([P, width_of(n)], F32, name="cand")
            nc.scalar.activation(out=cand[n][:], in_=gated[n][:], func=ACT.Tanh)

        def transpose_deter(n):
            c, j = units[n][0], units[n][1]
            deterT[n] = psum.tile([P, width_of(n)], F32, name="deterT", tag="bank")
            for i, b in enumerate(row_blocks(n)):
                nc.tensor.matmul(
                    out=deterT[n][:, i * P : (i + 1) * P],
                    lhsT=deter_sb[c][:, b, j * P : (j + 1) * P],
                    rhs=ident_bf16[:],
                    start=True,
                    stop=True,
                )

        def difference(n):
            diff[n] = work.tile([P, width_of(n)], F32, name="diff")
            nc.vector.tensor_tensor(out=diff[n][:], in0=cand[n][:], in1=deterT[n][:], op=ALU.subtract)

        def weighted_step(n):
            step[n] = work.tile([P, width_of(n)], F32, name="step")
            engine = nc.vector if n >= UNITS - VECTOR_STEPS else nc.gpsimd
            engine.tensor_tensor(out=step[n][:], in0=update[n][:], in1=diff[n][:], op=ALU.mult)

        def transpose_step(n):
            c, j = units[n][0], units[n][1]
            stepT[n] = psum.tile([P, width_of(n) // P, P], F32, name="stepT", tag="bank")
            for i, b in enumerate(row_blocks(n)):
                if on_scalar(n):
                    nc.tensor.matmul(
                        out=stepT[n][:, i, :],
                        lhsT=ident_bf16[:],
                        rhs=deter_sb[c][:, b, j * P : (j + 1) * P],
                        start=True,
                        stop=False,
                    )
                    nc.tensor.matmul(
                        out=stepT[n][:, i, :],
                        lhsT=step[n][:, i * P : (i + 1) * P],
                        rhs=ident_f32[:],
                        is_transpose=True,
                        start=False,
                        stop=True,
                    )
                else:
                    nc.tensor.transpose(stepT[n][:, i, :], step[n][:, i * P : (i + 1) * P], ident_f32[:])

        def blend_and_store(n):
            c, j = units[n][0], units[n][1]
            feats = slice(j * P, (j + 1) * P)
            rows = slice(row_blocks(n).start, row_blocks(n).stop)
            result = outs.tile([P, width_of(n) // P, P], F32, name="result")
            if on_scalar(n):
                nc.scalar.copy(out=result[:], in_=stepT[n][:])
            else:
                nc.vector.tensor_tensor(out=result[:], in0=stepT[n][:], in1=deter_sb[c][:, rows, feats], op=ALU.add)
            nc.sync.dma_start(out=chunk_rows(out, c)[:, rows, feats], in_=result[:])

        def at(stage, n):
            if 0 <= n < UNITS:
                stage(n)

        for c in range(2):
            for prepare_step in range(PREPARE_STEPS):
                prepare_on_tensor(c, prepare_step)
                prepare_elsewhere(c, prepare_step)

        bias_ps = psum.tile([P, P], BF16, tag="bank")
        nc.tensor.transpose(bias_ps[:], bias_rows[:], ident_bf16[:])
        bias_cols = keep.tile([P, GATES * FEATS], F32)
        nc.vector.tensor_copy(out=bias_cols[:], in_=bias_ps[:, 0 : GATES * FEATS])
        update_cols = bias_cols[:, UPDATE * FEATS : (UPDATE + 1) * FEATS]
        nc.vector.tensor_scalar_add(out=update_cols, in0=update_cols, scalar1=-1.0)
        for t in range(UNITS + LAG_OUT):
            load_later(t)
            if not on_scalar(t - LAG_OUT):
                at(blend_and_store, t - LAG_OUT)
            at(project, t)
            at(transpose_deter, t - LAG_CAND)
            at(transpose_step, t - LAG_BACK)
            prepare_on_tensor(2 + t // PREPARE_STEPS, t % PREPARE_STEPS)
            at(reset_gate, t)
            at(candidate, t - LAG_CAND)
            if t != UNITS - 1:
                at(update_gate, t)
            if t == UNITS:
                update_gate(UNITS - 1)
            if on_scalar(t - LAG_OUT):
                blend_and_store(t - LAG_OUT)
            at(gate_candidate, t)
            at(difference, t - LAG_CAND)
            at(weighted_step, t - LAG_CAND)
            prepare_elsewhere(2 + t // PREPARE_STEPS, t % PREPARE_STEPS)
